import numpy as np
import ml_dtypes

BF16 = ml_dtypes.bfloat16


def bf(x):
    return np.asarray(x, np.float32).astype(BF16)


def f32(x):
    return np.asarray(x, np.float32)


def f64(x):
    return np.asarray(x).astype(np.float64)


def striped(idx):
    return np.tile(idx.reshape(-1, 16).T, (8, 1))


S, K, D, N = 4096, 128, 128, 8192
WIDTH = 1.5


def make_smooth():
    pos = np.arange(S) * (K - 1.0) / (S - 1.0)
    dist = np.abs(pos[:, None] - np.arange(K)[None, :])
    wt = np.maximum(1.0 - dist / WIDTH, 0.0)
    return wt / wt.sum(axis=1, keepdims=True)


def setup_inputs():
    return {"smooth": bf(make_smooth()), "embed": bf(np.random.standard_normal((K, D))), "offs": striped(np.random.permutation(np.tile(np.arange(S), 2))[:N])}


def reference(smooth, embed, offs):
    idx = offs[:16].T.reshape(-1)
    return f64(embed).T @ f64(smooth)[idx].T

@@ -1,0 +1,53 @@
+import concourse.mybir as mybir
+from concourse.masks import make_identity
+
+P = 128
+S, K, D, N = 4096, 128, 128, 8192
+PIECE = 512
+BLOCKS = S // P
+CHUNK = 8
+BF16, F32, U16 = mybir.dt.bfloat16, mybir.dt.float32, mybir.dt.uint16
+
+FLOPS = 2 * K * D * N
+
+
+def tile_smoothembedding_kernel(tc, smooth, embed, offs, out):
+    nc = tc.nc
+    with (
+        tc.tile_pool(name="held", bufs=1) as held,
+        tc.psum_pool(name="flip_psum", bufs=2) as flip_psum,
+        tc.psum_pool(name="product_psum", bufs=4) as product_psum,
+    ):
+        rows = held.tile([P, BLOCKS, K], BF16, name="rows")
+        smooth_blocks = smooth.rearrange("(b p) k -> p b k", p=P)
+        for c in range(BLOCKS // CHUNK):
+            queue = nc.sync if c % 2 == 0 else nc.scalar
+            queue.dma_start(rows[:, c * CHUNK : (c + 1) * CHUNK, :], smooth_blocks[:, c * CHUNK : (c + 1) * CHUNK, :])
+        offsets = held.tile([P, N // 16], U16, name="offsets")
+        nc.sync.dma_start(offsets[:], offs)
+        weights = held.tile([K, D], BF16, name="weights")
+        nc.scalar.dma_start(weights[:], embed)
+
+        identity = held.tile([P, P], BF16, name="identity")
+        make_identity(nc, identity[:])
+
+        table = held.tile([K, S], BF16, name="table")
+        for c in range(BLOCKS // CHUNK):
+            flipped = flip_psum.tile([K, CHUNK * P], BF16, name="flipped")
+            for i in range(CHUNK):
+                nc.tensor.transpose(flipped[:, i * P : (i + 1) * P], rows[:, c * CHUNK + i, :], identity[:])
+            if c % 2 == 0:
+                nc.vector.tensor_copy(table[:, c * CHUNK * P : (c + 1) * CHUNK * P], flipped[:])
+            else:
+                nc.scalar.copy(table[:, c * CHUNK * P : (c + 1) * CHUNK * P], flipped[:])
+
+        staged = held.tile([D, N], F32, name="staged")
+        for u in range(N // PIECE):
+            product = product_psum.tile([D, PIECE], F32, name="product")
+            looked_up = table[:].indirect(offsets[:, u * (PIECE // 16) : (u + 1) * (PIECE // 16)])
+            nc.tensor.matmul(product[:], weights[:], looked_up, start=True, stop=True)
+            if u % 2 == 0:
+                nc.vector.tensor_copy(staged[:, u * PIECE : (u + 1) * PIECE], product[:])
+            else:
+                nc.scalar.copy(staged[:, u * PIECE : (u + 1) * PIECE], product[:])
+            nc.sync.dma_start(out[:, u * PIECE : (u + 1) * PIECE], staged[:, u * PIECE : (u + 1) * PIECE])

@@ -4,8 +4,8 @@ from concourse.masks import make_identity
 P = 128
 S, K, D, N = 4096, 128, 128, 8192
 PIECE = 512
-BLOCKS = S // P
-CHUNK = 8
+RUN = 4
+CHUNK = RUN * P
 BF16, F32, U16 = mybir.dt.bfloat16, mybir.dt.float32, mybir.dt.uint16
 
 FLOPS = 2 * K * D * N
@@ -15,14 +15,14 @@ def tile_smoothembedding_kernel(tc, smooth, embed, offs, out):
     nc = tc.nc
     with (
         tc.tile_pool(name="held", bufs=1) as held,
-        tc.psum_pool(name="flip_psum", bufs=2) as flip_psum,
+        tc.psum_pool(name="flip_psum", bufs=4) as flip_psum,
         tc.psum_pool(name="product_psum", bufs=4) as product_psum,
     ):
-        rows = held.tile([P, BLOCKS, K], BF16, name="rows")
-        smooth_blocks = smooth.rearrange("(b p) k -> p b k", p=P)
-        for c in range(BLOCKS // CHUNK):
+        rows = held.tile([P, S // CHUNK, RUN, K], BF16, name="rows")
+        smooth_chunks = smooth.rearrange("(c p i) k -> c p i k", p=P, i=RUN)
+        for c in range(S // CHUNK):
             queue = nc.sync if c % 2 == 0 else nc.scalar
-            queue.dma_start(rows[:, c * CHUNK : (c + 1) * CHUNK, :], smooth_blocks[:, c * CHUNK : (c + 1) * CHUNK, :])
+            queue.dma_start(rows[:, c, :, :], smooth_chunks[c])
         offsets = held.tile([P, N // 16], U16, name="offsets")
         nc.sync.dma_start(offsets[:], offs)
         weights = held.tile([K, D], BF16, name="weights")
@@ -32,14 +32,16 @@ def tile_smoothembedding_kernel(tc, smooth, embed, offs, out):
         make_identity(nc, identity[:])
 
         table = held.tile([K, S], BF16, name="table")
-        for c in range(BLOCKS // CHUNK):
-            flipped = flip_psum.tile([K, CHUNK * P], BF16, name="flipped")
-            for i in range(CHUNK):
-                nc.tensor.transpose(flipped[:, i * P : (i + 1) * P], rows[:, c * CHUNK + i, :], identity[:])
+        for c in range(S // CHUNK):
+            flipped = flip_psum.tile([K, RUN, P], BF16, name="flipped")
+            for i in range(RUN):
+                nc.tensor.transpose(flipped[:, i, :], rows[:, c, i, :], identity[:])
+            in_order = flipped[:].rearrange("k i p -> k p i")
+            columns = table[:, c * CHUNK : (c + 1) * CHUNK].rearrange("k (p i) -> k p i", i=RUN)
             if c % 2 == 0:
-                nc.vector.tensor_copy(table[:, c * CHUNK * P : (c + 1) * CHUNK * P], flipped[:])
+                nc.vector.tensor_copy(columns, in_order)
             else:
-                nc.scalar.copy(table[:, c * CHUNK * P : (c + 1) * CHUNK * P], flipped[:])
+                nc.scalar.copy(columns, in_order)
 
         staged = held.tile([D, N], F32, name="staged")
         for u in range(N // PIECE):

@@ -15,7 +15,8 @@ def tile_smoothembedding_kernel(tc, smooth, embed, offs, out):
     nc = tc.nc
     with (
         tc.tile_pool(name="held", bufs=1) as held,
-        tc.psum_pool(name="flip_psum", bufs=4) as flip_psum,
+        tc.psum_pool(name="flip_psum", bufs=3) as flip_psum,
+        tc.psum_pool(name="idle_psum", bufs=1) as idle_psum,
         tc.psum_pool(name="product_psum", bufs=4) as product_psum,
     ):
         rows = held.tile([P, S // CHUNK, RUN, K], BF16, name="rows")
@@ -31,11 +32,19 @@ def tile_smoothembedding_kernel(tc, smooth, embed, offs, out):
         identity = held.tile([P, P], BF16, name="identity")
         make_identity(nc, identity[:])
 
+        zeros = held.tile([P, PIECE], BF16, name="zeros")
+        nc.vector.memset(zeros[:], 0.0)
+        unread = idle_psum.tile([P, PIECE], F32, name="unread")
+        for repeat in range(4):
+            nc.tensor.matmul(unread[:], zeros[:, 0:P], zeros[:], start=True, stop=True)
+
         table = held.tile([K, S], BF16, name="table")
         for c in range(S // CHUNK):
             flipped = flip_psum.tile([K, RUN, P], BF16, name="flipped")
             for i in range(RUN):
                 nc.tensor.transpose(flipped[:, i, :], rows[:, c, i, :], identity[:])
+            if c % 2 == 1:
+                nc.tensor.matmul(unread[:], identity[:], rows[:, c, :, :].rearrange("p i k -> p (i k)"), start=True, stop=True)
             in_order = flipped[:].rearrange("k i p -> k p i")
             columns = table[:, c * CHUNK : (c + 1) * CHUNK].rearrange("k (p i) -> k p i", i=RUN)
             if c % 2 == 0:

import concourse.mybir as mybir
from concourse.masks import make_identity

P = 128
S, K, D, N = 4096, 128, 128, 8192
PIECE = 512
RUN = 4
CHUNK = RUN * P
BF16, F32, U16 = mybir.dt.bfloat16, mybir.dt.float32, mybir.dt.uint16

FLOPS = 2 * K * D * N


def tile_smoothembedding_kernel(tc, smooth, embed, offs, out):
    nc = tc.nc
    with (
        tc.tile_pool(name="held", bufs=1) as held,
        tc.psum_pool(name="flip_psum", bufs=3) as flip_psum,
        tc.psum_pool(name="idle_psum", bufs=1) as idle_psum,
        tc.psum_pool(name="product_psum", bufs=4) as product_psum,
    ):
        rows = held.tile([P, S // CHUNK, RUN, K], BF16, name="rows")
        smooth_chunks = smooth.rearrange("(c p i) k -> c p i k", p=P, i=RUN)
        for c in range(S // CHUNK):
            queue = nc.sync if c % 2 == 0 else nc.scalar
            queue.dma_start(rows[:, c, :, :], smooth_chunks[c])
        offsets = held.tile([P, N // 16], U16, name="offsets")
        nc.sync.dma_start(offsets[:], offs)
        weights = held.tile([K, D], BF16, name="weights")
        nc.scalar.dma_start(weights[:], embed)

        identity = held.tile([P, P], BF16, name="identity")
        make_identity(nc, identity[:])

        zeros = held.tile([P, PIECE], BF16, name="zeros")
        nc.vector.memset(zeros[:], 0.0)
        unread = idle_psum.tile([P, PIECE], F32, name="unread")
        for repeat in range(4):
            nc.tensor.matmul(unread[:], zeros[:, 0:P], zeros[:], start=True, stop=True)

        table = held.tile([K, S], BF16, name="table")
        for c in range(S // CHUNK):
            flipped = flip_psum.tile([K, RUN, P], BF16, name="flipped")
            for i in range(RUN):
                nc.tensor.transpose(flipped[:, i, :], rows[:, c, i, :], identity[:])
            if c % 2 == 1:
                nc.tensor.matmul(unread[:], identity[:], rows[:, c, :, :].rearrange("p i k -> p (i k)"), start=True, stop=True)
            in_order = flipped[:].rearrange("k i p -> k p i")
            columns = table[:, c * CHUNK : (c + 1) * CHUNK].rearrange("k (p i) -> k p i", i=RUN)
            if c % 2 == 0:
                nc.vector.tensor_copy(columns, in_order)
            else:
                nc.scalar.copy(columns, in_order)

        staged = held.tile([D, N], F32, name="staged")
        for u in range(N // PIECE):
            product = product_psum.tile([D, PIECE], F32, name="product")
            looked_up = table[:].indirect(offsets[:, u * (PIECE // 16) : (u + 1) * (PIECE // 16)])
            nc.tensor.matmul(product[:], weights[:], looked_up, start=True, stop=True)
            if u % 2 == 0:
                nc.vector.tensor_copy(staged[:, u * PIECE : (u + 1) * PIECE], product[:])
            else:
                nc.scalar.copy(staged[:, u * PIECE : (u + 1) * PIECE], product[:])
            nc.sync.dma_start(out[:, u * PIECE : (u + 1) * PIECE], staged[:, u * PIECE : (u + 1) * PIECE])
